import numpy as np
import ml_dtypes


def mxq(x, axis, fmt="e4m3"):
    dtype, down = {"e4m3": (ml_dtypes.float8_e4m3fn, 7), "e5m2": (ml_dtypes.float8_e5m2, 14)}[fmt]
    v = np.moveaxis(np.asarray(x, np.float32).astype(ml_dtypes.bfloat16).astype(np.float64), axis, -1)
    blocks = v.reshape(v.shape[:-1] + (-1, 32))
    amax = np.abs(blocks).max(-1, keepdims=True)
    byte = np.maximum(np.where(amax > 0, np.frexp(amax)[1] - 1 + 127, 0) - down, 1)
    scale = np.exp2(byte - 127.0)
    codes = (blocks / scale).astype(np.float32).astype(dtype).astype(np.float64)
    return np.moveaxis((codes * scale).reshape(v.shape), -1, axis)


WIDE = False


def mx_kscale(k):
    if not WIDE:
        return np.ones(k)
    levels = np.array([10, -10, 5, -5, 0])
    a = np.random.permutation(np.resize(levels, k // 512 * 4)).reshape(k // 512, 4)
    idx = np.arange(k)
    return np.exp2(a[idx // 512, idx % 128 // 32])


BF16 = ml_dtypes.bfloat16


def bf(x):
    return np.asarray(x, np.float32).astype(BF16)


def f64(x):
    return np.asarray(x).astype(np.float64)


E2M1 = np.array([0.0, 0.5, 1.0, 1.5, 2.0, 3.0, 4.0, 6.0, -0.0, -0.5, -1.0, -1.5, -2.0, -3.0, -4.0, -6.0])


def pack_weight(w, fmt):
    k, n = w.shape
    w = f64(bf(w)).reshape(k // 32, 32, n)
    amax = np.abs(w).max(1)
    if fmt == "e4m3":
        byte = np.frexp(amax)[1] - 1 + 127 - 7
    else:
        mant, ex = np.frexp(amax / 6.0)
        byte = np.where(mant > 0.5, ex, ex - 1) + 127
    byte = np.clip(np.where(amax > 0, byte, 1), 1, 254)
    scaled = (w * np.exp2(127.0 - byte)[:, None, :]).reshape(k, n).astype(np.float32)
    by_word = np.ascontiguousarray(scaled.reshape(k // 512, 128, 4, n).transpose(0, 1, 3, 2))
    if fmt == "e4m3":
        words = by_word.astype(ml_dtypes.float8_e4m3fn).view(np.uint8)
    else:
        c = by_word.astype(ml_dtypes.float4_e2m1fn).view(np.uint8) & 0xF
        words = c[..., 0::2] | (c[..., 1::2] << 4)
    return np.ascontiguousarray(words), np.ascontiguousarray(byte.astype(np.uint8).reshape(k // 512, 16, n))


def unpack_weight(words, scales, fmt):
    g, p, n, _ = words.shape
    if fmt == "e4m3":
        vals = np.ascontiguousarray(words).view(ml_dtypes.float8_e4m3fn).astype(np.float64)
    else:
        nib = np.empty((g, p, n, 4), np.uint8)
        nib[..., 0::2] = words & 0xF
        nib[..., 1::2] = words >> 4
        vals = E2M1[nib]
    vals = vals * np.repeat(np.exp2(scales.astype(np.float64) - 127.0), 8, axis=1)[..., None]
    return vals.transpose(0, 1, 3, 2).reshape(g * 512, n)

def pack4(w):
    words, scales = pack_weight(w, "e2m1")
    return words.reshape(words.shape[0], 128, -1), scales


def unpack4(words, scales):
    return unpack_weight(words.reshape(words.shape[0], 128, -1, 2), scales, "e2m1")


B, S, HID, H, D = 1, 1024, 1024, 8, 128
QKV = 3 * H * D


def rotate_half(x):
    x1, x2 = x[..., : x.shape[-1] // 2], x[..., x.shape[-1] // 2 :]
    return np.concatenate((-x2, x1), axis=-1)


def setup_inputs():
    s = mx_kscale(HID)
    hidden_states = bf(np.random.standard_normal((B, S, HID)) * s)
    cos = bf(np.random.uniform(size=(S, D)))
    sin = bf(np.random.uniform(size=(S, D)))
    words, scales = pack4(np.random.standard_normal((HID, QKV)) * 2.0 / np.sqrt(HID) / s[:, None])
    return {"hidden_states": hidden_states,
            "cos": cos,
            "sin": sin,
            "w_qkv_words": words,
            "w_qkv_scales": scales}


def reference(hidden_states, cos, sin, w_qkv_words, w_qkv_scales):
    qkv = mxq(f64(hidden_states), 2, "e4m3") @ unpack4(w_qkv_words, w_qkv_scales)
    qkv = qkv.reshape(B, S, 3 * H, D)
    q, k, v = qkv[:, :, :H], qkv[:, :, H:2 * H], qkv[:, :, 2 * H:]
    c = f64(cos)[:, None, :]
    sn = f64(sin)[:, None, :]
    q_rot = q * c + rotate_half(q) * sn
    k_rot = k * c + rotate_half(k) * sn
    return q_rot, k_rot, v

@@ -1,0 +1,163 @@
+from contextlib import ExitStack
+
+import concourse.mybir as mybir
+from concourse.masks import make_identity
+
+F32 = mybir.dt.float32
+BF16 = mybir.dt.bfloat16
+I32 = mybir.dt.int32
+U32 = mybir.dt.uint32
+U8 = mybir.dt.uint8
+FP8X4 = mybir.dt.float8_e4m3fn_x4
+FP4X4 = mybir.dt.float4_e2m1fn_x4
+ALU = mybir.AluOpType
+
+P = 128
+PACK = 4
+K_PASS = P * PACK
+TOKENS = 1024
+HID = 1024
+HEADS = 8
+D = 128
+HALF = D // 2
+QKV = 3 * HEADS * D
+TOKEN_TILES = TOKENS // P
+PASSES = HID // K_PASS
+BANK = 512
+HEADS_PER_BANK = BANK // D
+BANKS_PER_OUTPUT = HEADS // HEADS_PER_BANK
+
+FLOPS = 2 * TOKENS * HID * QKV
+
+
+def tile_attention_pa_kernel(
+    tc, hidden_states, cos, sin, w_qkv_words, w_qkv_scales, out_0, out_1, out_2
+):
+    nc = tc.nc
+
+    x_dram = hidden_states[0].rearrange("(p t) k -> p t k", t=TOKEN_TILES)
+    cos_dram = cos.rearrange("(p t) d -> p t d", t=TOKEN_TILES)
+    sin_dram = sin.rearrange("(p t) d -> p t d", t=TOKEN_TILES)
+    outs = [
+        o[0].rearrange("(p t) h d -> p t (h d)", t=TOKEN_TILES) for o in (out_0, out_1, out_2)
+    ]
+
+    with ExitStack() as ctx:
+        keep = ctx.enter_context(tc.tile_pool(name="keep", bufs=1))
+        stage = ctx.enter_context(tc.tile_pool(name="stage", bufs=3))
+        results = ctx.enter_context(tc.tile_pool(name="results", bufs=4))
+        xt_psum = ctx.enter_context(tc.psum_pool(name="xt_psum", bufs=2))
+        acc_psum = ctx.enter_context(tc.psum_pool(name="acc_psum", bufs=6))
+
+        w_scales = keep.tile([P, PASSES, QKV], U8, align_bytes=64)
+        nc.vector.memset(w_scales[:].rearrange("p g n -> p (g n)").bitcast(I32), 0)
+
+        x_sb = keep.tile([P, TOKEN_TILES, HID], BF16)
+        nc.sync.dma_start(out=x_sb[:, 0, :], in_=x_dram[:, 0, :])
+
+        for b in range(2):
+            for r in range(4):
+                nc.sync.dma_start(
+                    out=w_scales[32 * b + r : P : 64, :, :].bitcast(I32),
+                    in_=w_qkv_scales[:, 4 * b + r : 16 : 8, :]
+                    .rearrange("g q n -> q g n")
+                    .bitcast(I32),
+                )
+
+        w_words = keep.tile([P, PASSES, 2 * QKV], U8, align_bytes=64)
+        cos_sb = keep.tile([P, TOKEN_TILES, D], BF16)
+        sin_sb = keep.tile([P, TOKEN_TILES, D], BF16)
+
+        def load_words(o):
+            cols = slice(2 * HEADS * D * o, 2 * HEADS * D * (o + 1))
+            nc.sync.dma_start(
+                out=w_words[:, :, cols].bitcast(I32),
+                in_=w_qkv_words[:, :, cols].rearrange("g p n -> p g n").bitcast(I32),
+            )
+
+        load_words(0)
+        nc.sync.dma_start(out=cos_sb[:], in_=cos_dram)
+        nc.sync.dma_start(out=sin_sb[:], in_=sin_dram)
+        load_words(1)
+        load_words(2)
+        for t in range(1, TOKEN_TILES):
+            nc.sync.dma_start(out=x_sb[:, t, :], in_=x_dram[:, t, :])
+
+        ident = keep.tile([P, P], F32)
+        make_identity(nc, ident[:])
+
+        x_codes = keep.tile([P, TOKEN_TILES, PASSES * P], U32, align_bytes=64)
+        x_scales = keep.tile([P, TOKEN_TILES, PASSES * P], U8, align_bytes=64)
+
+        def prepare(t):
+            x_words = x_sb[:, t, :].bitcast(F32)
+            xt = xt_psum.tile([P, PASSES, 2, P], F32)
+            for g in range(PASSES):
+                for u in range(2):
+                    nc.tensor.transpose(
+                        xt[:, g, u, :], x_words[:, 256 * g + u : 256 * (g + 1) : 2], ident[:]
+                    )
+            grouped = stage.tile([P, PASSES * P * PACK], BF16, align_bytes=64)
+            nc.scalar.copy(
+                out=grouped[:].bitcast(F32).rearrange("p (g r u) -> p g r u", g=PASSES, u=2),
+                in_=xt[:].rearrange("p g u r -> p g r u"),
+            )
+            nc.vector.quantize_mx(
+                out=x_codes[:, t, :].bitcast(FP8X4), scales=x_scales[:, t, :], in_=grouped[:]
+            )
+
+        def project(t, c):
+            acc = acc_psum.tile([P, BANK], F32)
+            for g in range(PASSES):
+                nc.tensor.matmul_mx(
+                    out=acc[:],
+                    lhsT=x_codes[:, t, P * g : P * (g + 1)].bitcast(FP8X4),
+                    lhsT_scale=x_scales[:, t, P * g : P * (g + 1)],
+                    rhs=w_words[:, g, 2 * BANK * c : 2 * BANK * (c + 1)].bitcast(FP4X4),
+                    rhs_scale=w_scales[:, g, BANK * c : BANK * (c + 1)],
+                    start=(g == 0),
+                    stop=(g == PASSES - 1),
+                )
+            return acc
+
+        prepare(0)
+
+        tables = keep.tile([P, TOKEN_TILES, 2, D], BF16)
+        nc.vector.tensor_copy(out=tables[:, :, 0, :], in_=cos_sb[:])
+        nc.vector.tensor_copy(out=tables[:, :, 1, 0:HALF], in_=sin_sb[:, :, HALF:D])
+        nc.vector.tensor_copy(out=tables[:, :, 1, HALF:D], in_=sin_sb[:, :, 0:HALF])
+
+        shape = [P, 2, HEADS_PER_BANK, D]
+        for t in range(TOKEN_TILES):
+            if t + 1 < TOKEN_TILES:
+                prepare(t + 1)
+            for o in range(2):
+                products = results.tile([P, 2, HEADS, D], F32)
+                for b in range(BANKS_PER_OUTPUT):
+                    acc = project(t, BANKS_PER_OUTPUT * o + b)
+                    nc.vector.tensor_tensor(
+                        out=products[:, :, HEADS_PER_BANK * b : HEADS_PER_BANK * (b + 1), :],
+                        in0=acc[:].rearrange("p (h d) -> p h d", d=D).unsqueeze(1).to_broadcast(shape),
+                        in1=tables[:, t, :, :].unsqueeze(2).to_broadcast(shape),
+                        op=ALU.mult,
+                    )
+                direct = products[:, 0, :, :]
+                crossed = products[:, 1, :, :]
+                nc.gpsimd.tensor_tensor(
+                    out=direct[:, :, 0:HALF],
+                    in0=direct[:, :, 0:HALF],
+                    in1=crossed[:, :, HALF:D],
+                    op=ALU.subtract,
+                )
+                nc.gpsimd.tensor_tensor(
+                    out=direct[:, :, HALF:D],
+                    in0=direct[:, :, HALF:D],
+                    in1=crossed[:, :, 0:HALF],
+                    op=ALU.add,
+                )
+                nc.sync.dma_start(out=outs[o][:, t, :], in_=direct.rearrange("p h d -> p (h d)"))
+            v_sb = results.tile([P, HEADS * D], F32)
+            for b in range(BANKS_PER_OUTPUT):
+                acc = project(t, BANKS_PER_OUTPUT * 2 + b)
+                nc.scalar.copy(out=v_sb[:, BANK * b : BANK * (b + 1)], in_=acc[:])
+            nc.sync.dma_start(out=outs[2][:, t, :], in_=v_sb[:])

@@ -38,9 +38,10 @@ def tile_attention_pa_kernel(
     x_dram = hidden_states[0].rearrange("(p t) k -> p t k", t=TOKEN_TILES)
     cos_dram = cos.rearrange("(p t) d -> p t d", t=TOKEN_TILES)
     sin_dram = sin.rearrange("(p t) d -> p t d", t=TOKEN_TILES)
-    outs = [
-        o[0].rearrange("(p t) h d -> p t (h d)", t=TOKEN_TILES) for o in (out_0, out_1, out_2)
+    rotated_dram = [
+        o[0].rearrange("(p t) h d -> p t (h d)", t=TOKEN_TILES) for o in (out_0, out_1)
     ]
+    v_dram = out_2[0].rearrange("(p t) h d -> p t (h d)", t=TOKEN_TILES)
 
     with ExitStack() as ctx:
         keep = ctx.enter_context(tc.tile_pool(name="keep", bufs=1))
@@ -49,45 +50,46 @@ def tile_attention_pa_kernel(
         xt_psum = ctx.enter_context(tc.psum_pool(name="xt_psum", bufs=2))
         acc_psum = ctx.enter_context(tc.psum_pool(name="acc_psum", bufs=6))
 
+        x_sb = keep.tile([P, TOKEN_TILES, HID], BF16)
+        cos_sb = keep.tile([P, TOKEN_TILES, D], BF16)
+        sin_sb = keep.tile([P, TOKEN_TILES, D], BF16)
+        w_words = keep.tile([P, QKV // BANK, PASSES, 2 * BANK], U8, align_bytes=64)
         w_scales = keep.tile([P, PASSES, QKV], U8, align_bytes=64)
         nc.vector.memset(w_scales[:].rearrange("p g n -> p (g n)").bitcast(I32), 0)
 
-        x_sb = keep.tile([P, TOKEN_TILES, HID], BF16)
-        nc.sync.dma_start(out=x_sb[:, 0, :], in_=x_dram[:, 0, :])
+        def load_x(t):
+            nc.sync.dma_start(out=x_sb[:, t, :], in_=x_dram[:, t, :])
 
-        for b in range(2):
-            for r in range(4):
-                nc.sync.dma_start(
-                    out=w_scales[32 * b + r : P : 64, :, :].bitcast(I32),
-                    in_=w_qkv_scales[:, 4 * b + r : 16 : 8, :]
-                    .rearrange("g q n -> q g n")
-                    .bitcast(I32),
-                )
-
-        w_words = keep.tile([P, PASSES, 2 * QKV], U8, align_bytes=64)
-        cos_sb = keep.tile([P, TOKEN_TILES, D], BF16)
-        sin_sb = keep.tile([P, TOKEN_TILES, D], BF16)
-
-        def load_words(o):
-            cols = slice(2 * HEADS * D * o, 2 * HEADS * D * (o + 1))
+        def load_words(c):
             nc.sync.dma_start(
-                out=w_words[:, :, cols].bitcast(I32),
-                in_=w_qkv_words[:, :, cols].rearrange("g p n -> p g n").bitcast(I32),
+                out=w_words[:, c, :, :].bitcast(I32),
+                in_=w_qkv_words[:, :, 2 * BANK * c : 2 * BANK * (c + 1)]
+                .rearrange("g p n -> p g n")
+                .bitcast(I32),
             )
 
+        load_x(0)
+        for r in range(4):
+            nc.sync.dma_start(
+                out=w_scales[r:P:32, :, :].bitcast(I32),
+                in_=w_qkv_scales[:, r:16:4, :].rearrange("g q n -> q g n").bitcast(I32),
+            )
         load_words(0)
-        nc.sync.dma_start(out=cos_sb[:], in_=cos_dram)
         nc.sync.dma_start(out=sin_sb[:], in_=sin_dram)
+        nc.sync.dma_start(out=cos_sb[:], in_=cos_dram)
         load_words(1)
-        load_words(2)
-        for t in range(1, TOKEN_TILES):
-            nc.sync.dma_start(out=x_sb[:, t, :], in_=x_dram[:, t, :])
+        load_x(1)
+        for c in range(2, QKV // BANK):
+            load_words(c)
+        for t in range(2, TOKEN_TILES):
+            load_x(t)
 
         ident = keep.tile([P, P], F32)
         make_identity(nc, ident[:])
 
         x_codes = keep.tile([P, TOKEN_TILES, PASSES * P], U32, align_bytes=64)
         x_scales = keep.tile([P, TOKEN_TILES, PASSES * P], U8, align_bytes=64)
+        factors = keep.tile([P, TOKEN_TILES, 2, D], BF16)
 
         def prepare(t):
             x_words = x_sb[:, t, :].bitcast(F32)
@@ -105,6 +107,10 @@ def tile_attention_pa_kernel(
             nc.vector.quantize_mx(
                 out=x_codes[:, t, :].bitcast(FP8X4), scales=x_scales[:, t, :], in_=grouped[:]
             )
+            nc.scalar.copy(out=factors[:, t, 0, 0:HALF], in_=cos_sb[:, t, 0:HALF])
+            nc.scalar.mul(out=factors[:, t, 0, HALF:D], in_=sin_sb[:, t, 0:HALF], mul=-1.0)
+            nc.scalar.copy(out=factors[:, t, 1, 0:HALF], in_=sin_sb[:, t, HALF:D])
+            nc.scalar.copy(out=factors[:, t, 1, HALF:D], in_=cos_sb[:, t, HALF:D])
 
         def project(t, c):
             acc = acc_psum.tile([P, BANK], F32)
@@ -113,7 +119,7 @@ def tile_attention_pa_kernel(
                     out=acc[:],
                     lhsT=x_codes[:, t, P * g : P * (g + 1)].bitcast(FP8X4),
                     lhsT_scale=x_scales[:, t, P * g : P * (g + 1)],
-                    rhs=w_words[:, g, 2 * BANK * c : 2 * BANK * (c + 1)].bitcast(FP4X4),
+                    rhs=w_words[:, c, g, :].bitcast(FP4X4),
                     rhs_scale=w_scales[:, g, BANK * c : BANK * (c + 1)],
                     start=(g == 0),
                     stop=(g == PASSES - 1),
@@ -122,42 +128,40 @@ def tile_attention_pa_kernel(
 
         prepare(0)
 
-        tables = keep.tile([P, TOKEN_TILES, 2, D], BF16)
-        nc.vector.tensor_copy(out=tables[:, :, 0, :], in_=cos_sb[:])
-        nc.vector.tensor_copy(out=tables[:, :, 1, 0:HALF], in_=sin_sb[:, :, HALF:D])
-        nc.vector.tensor_copy(out=tables[:, :, 1, HALF:D], in_=sin_sb[:, :, 0:HALF])
+        def rotate(t, o, adder):
+            shape = [P, 2, HEADS_PER_BANK, D]
+            products = results.tile([P, 2, HEADS, D], F32)
+            for b in range(BANKS_PER_OUTPUT):
+                acc = project(t, BANKS_PER_OUTPUT * o + b)
+                nc.vector.tensor_tensor(
+                    out=products[:, :, HEADS_PER_BANK * b : HEADS_PER_BANK * (b + 1), :],
+                    in0=acc[:].rearrange("p (h d) -> p h d", d=D).unsqueeze(1).to_broadcast(shape),
+                    in1=factors[:, t, :, :].unsqueeze(2).to_broadcast(shape),
+                    op=ALU.mult,
+                )
+            rotated = results.tile([P, HEADS, D], F32)
+            adder.tensor_tensor(
+                out=rotated[:].rearrange("p h (r j) -> p r h j", r=2),
+                in0=products[:, :, :, 0:HALF],
+                in1=products[:, :, :, HALF:D],
+                op=ALU.add,
+            )
+            nc.sync.dma_start(
+                out=rotated_dram[o][:, t, :], in_=rotated[:].rearrange("p h d -> p (h d)")
+            )
 
-        shape = [P, 2, HEADS_PER_BANK, D]
-        for t in range(TOKEN_TILES):
-            if t + 1 < TOKEN_TILES:
-                prepare(t + 1)
-            for o in range(2):
-                products = results.tile([P, 2, HEADS, D], F32)
-                for b in range(BANKS_PER_OUTPUT):
-                    acc = project(t, BANKS_PER_OUTPUT * o + b)
-                    nc.vector.tensor_tensor(
-                        out=products[:, :, HEADS_PER_BANK * b : HEADS_PER_BANK * (b + 1), :],
-                        in0=acc[:].rearrange("p (h d) -> p h d", d=D).unsqueeze(1).to_broadcast(shape),
-                        in1=tables[:, t, :, :].unsqueeze(2).to_broadcast(shape),
-                        op=ALU.mult,
-                    )
-                direct = products[:, 0, :, :]
-                crossed = products[:, 1, :, :]
-                nc.gpsimd.tensor_tensor(
-                    out=direct[:, :, 0:HALF],
-                    in0=direct[:, :, 0:HALF],
-                    in1=crossed[:, :, HALF:D],
-                    op=ALU.subtract,
-                )
-                nc.gpsimd.tensor_tensor(
-                    out=direct[:, :, HALF:D],
-                    in0=direct[:, :, HALF:D],
-                    in1=crossed[:, :, 0:HALF],
-                    op=ALU.add,
-                )
-                nc.sync.dma_start(out=outs[o][:, t, :], in_=direct.rearrange("p h d -> p (h d)"))
+        def copy_v(t):
             v_sb = results.tile([P, HEADS * D], F32)
             for b in range(BANKS_PER_OUTPUT):
                 acc = project(t, BANKS_PER_OUTPUT * 2 + b)
                 nc.scalar.copy(out=v_sb[:, BANK * b : BANK * (b + 1)], in_=acc[:])
-            nc.sync.dma_start(out=outs[2][:, t, :], in_=v_sb[:])
+            nc.scalar.dma_start(out=v_dram[:, t, :], in_=v_sb[:])
+
+        for t in range(TOKEN_TILES - 1):
+            rotate(t, 0, nc.gpsimd)
+            prepare(t + 1)
+            rotate(t, 1, nc.gpsimd)
+            copy_v(t)
+        rotate(TOKEN_TILES - 1, 0, nc.gpsimd)
+        copy_v(TOKEN_TILES - 1)
+        rotate(TOKEN_TILES - 1, 1, nc.vector)

@@ -45,10 +45,9 @@ def tile_attention_pa_kernel(
 
     with ExitStack() as ctx:
         keep = ctx.enter_context(tc.tile_pool(name="keep", bufs=1))
-        stage = ctx.enter_context(tc.tile_pool(name="stage", bufs=3))
+        stage = ctx.enter_context(tc.tile_pool(name="stage", bufs=4))
         results = ctx.enter_context(tc.tile_pool(name="results", bufs=4))
-        xt_psum = ctx.enter_context(tc.psum_pool(name="xt_psum", bufs=2))
-        acc_psum = ctx.enter_context(tc.psum_pool(name="acc_psum", bufs=6))
+        banks = ctx.enter_context(tc.psum_pool(name="banks", bufs=8))
 
         x_sb = keep.tile([P, TOKEN_TILES, HID], BF16)
         cos_sb = keep.tile([P, TOKEN_TILES, D], BF16)
@@ -68,21 +67,17 @@ def tile_attention_pa_kernel(
                 .bitcast(I32),
             )
 
-        load_x(0)
+        for t in range(TOKEN_TILES):
+            load_x(t)
+        nc.sync.dma_start(out=sin_sb[:], in_=sin_dram)
+        nc.sync.dma_start(out=cos_sb[:], in_=cos_dram)
         for r in range(4):
             nc.sync.dma_start(
                 out=w_scales[r:P:32, :, :].bitcast(I32),
                 in_=w_qkv_scales[:, r:16:4, :].rearrange("g q n -> q g n").bitcast(I32),
             )
-        load_words(0)
-        nc.sync.dma_start(out=sin_sb[:], in_=sin_dram)
-        nc.sync.dma_start(out=cos_sb[:], in_=cos_dram)
-        load_words(1)
-        load_x(1)
-        for c in range(2, QKV // BANK):
+        for c in range(QKV // BANK):
             load_words(c)
-        for t in range(2, TOKEN_TILES):
-            load_x(t)
 
         ident = keep.tile([P, P], F32)
         make_identity(nc, ident[:])
@@ -93,7 +88,7 @@ def tile_attention_pa_kernel(
 
         def prepare(t):
             x_words = x_sb[:, t, :].bitcast(F32)
-            xt = xt_psum.tile([P, PASSES, 2, P], F32)
+            xt = banks.tile([P, PASSES, 2, P], F32, tag="bank")
             for g in range(PASSES):
                 for u in range(2):
                     nc.tensor.transpose(
@@ -107,13 +102,9 @@ def tile_attention_pa_kernel(
             nc.vector.quantize_mx(
                 out=x_codes[:, t, :].bitcast(FP8X4), scales=x_scales[:, t, :], in_=grouped[:]
             )
-            nc.scalar.copy(out=factors[:, t, 0, 0:HALF], in_=cos_sb[:, t, 0:HALF])
-            nc.scalar.mul(out=factors[:, t, 0, HALF:D], in_=sin_sb[:, t, 0:HALF], mul=-1.0)
-            nc.scalar.copy(out=factors[:, t, 1, 0:HALF], in_=sin_sb[:, t, HALF:D])
-            nc.scalar.copy(out=factors[:, t, 1, HALF:D], in_=cos_sb[:, t, HALF:D])
 
         def project(t, c):
-            acc = acc_psum.tile([P, BANK], F32)
+            acc = banks.tile([P, BANK], F32, tag="bank")
             for g in range(PASSES):
                 nc.tensor.matmul_mx(
                     out=acc[:],
@@ -126,7 +117,12 @@ def tile_attention_pa_kernel(
                 )
             return acc
 
-        prepare(0)
+        for t in range(TOKEN_TILES):
+            prepare(t)
+        nc.vector.tensor_copy(out=factors[:, :, 0, 0:HALF], in_=cos_sb[:, :, 0:HALF])
+        nc.vector.tensor_scalar_mul(out=factors[:, :, 0, HALF:D], in0=sin_sb[:, :, 0:HALF], scalar1=-1.0)
+        nc.vector.tensor_copy(out=factors[:, :, 1, 0:HALF], in_=sin_sb[:, :, HALF:D])
+        nc.vector.tensor_copy(out=factors[:, :, 1, HALF:D], in_=cos_sb[:, :, HALF:D])
 
         def rotate(t, o, adder):
             shape = [P, 2, HEADS_PER_BANK, D]
@@ -159,7 +155,6 @@ def tile_attention_pa_kernel(
 
         for t in range(TOKEN_TILES - 1):
             rotate(t, 0, nc.gpsimd)
-            prepare(t + 1)
             rotate(t, 1, nc.gpsimd)
             copy_v(t)
         rotate(TOKEN_TILES - 1, 0, nc.gpsimd)

@@ -124,7 +124,7 @@ def tile_attention_pa_kernel(
         nc.vector.tensor_copy(out=factors[:, :, 1, 0:HALF], in_=sin_sb[:, :, HALF:D])
         nc.vector.tensor_copy(out=factors[:, :, 1, HALF:D], in_=cos_sb[:, :, HALF:D])
 
-        def rotate(t, o, adder):
+        def multiply(t, o):
             shape = [P, 2, HEADS_PER_BANK, D]
             products = results.tile([P, 2, HEADS, D], F32)
             for b in range(BANKS_PER_OUTPUT):
@@ -135,16 +135,22 @@ def tile_attention_pa_kernel(
                     in1=factors[:, t, :, :].unsqueeze(2).to_broadcast(shape),
                     op=ALU.mult,
                 )
+            return products
+
+        def add_and_store(t, o, products, adder, pieces):
             rotated = results.tile([P, HEADS, D], F32)
-            adder.tensor_tensor(
-                out=rotated[:].rearrange("p h (r j) -> p r h j", r=2),
-                in0=products[:, :, :, 0:HALF],
-                in1=products[:, :, :, HALF:D],
-                op=ALU.add,
-            )
-            nc.sync.dma_start(
-                out=rotated_dram[o][:, t, :], in_=rotated[:].rearrange("p h d -> p (h d)")
-            )
+            step = HEADS // pieces
+            for h in range(0, HEADS, step):
+                adder.tensor_tensor(
+                    out=rotated[:, h : h + step, :].rearrange("p h (r j) -> p r h j", r=2),
+                    in0=products[:, :, h : h + step, 0:HALF],
+                    in1=products[:, :, h : h + step, HALF:D],
+                    op=ALU.add,
+                )
+                nc.sync.dma_start(
+                    out=rotated_dram[o][:, t, D * h : D * (h + step)],
+                    in_=rotated[:, h : h + step, :].rearrange("p h d -> p (h d)"),
+                )
 
         def copy_v(t):
             v_sb = results.tile([P, HEADS * D], F32)
@@ -154,9 +160,12 @@ def tile_attention_pa_kernel(
             nc.scalar.dma_start(out=v_dram[:, t, :], in_=v_sb[:])
 
         for t in range(TOKEN_TILES - 1):
-            rotate(t, 0, nc.gpsimd)
-            rotate(t, 1, nc.gpsimd)
+            for o in range(2):
+                add_and_store(t, o, multiply(t, o), nc.gpsimd, 1)
             copy_v(t)
-        rotate(TOKEN_TILES - 1, 0, nc.gpsimd)
-        copy_v(TOKEN_TILES - 1)
-        rotate(TOKEN_TILES - 1, 1, nc.vector)
+        last = TOKEN_TILES - 1
+        last_q = multiply(last, 0)
+        copy_v(last)
+        last_k = multiply(last, 1)
+        add_and_store(last, 0, last_q, nc.vector, 1)
+        add_and_store(last, 1, last_k, nc.vector, 2)

@@ -53,8 +53,11 @@ def tile_attention_pa_kernel(
         cos_sb = keep.tile([P, TOKEN_TILES, D], BF16)
         sin_sb = keep.tile([P, TOKEN_TILES, D], BF16)
         w_words = keep.tile([P, QKV // BANK, PASSES, 2 * BANK], U8, align_bytes=64)
-        w_scales = keep.tile([P, PASSES, QKV], U8, align_bytes=64)
-        nc.vector.memset(w_scales[:].rearrange("p g n -> p (g n)").bitcast(I32), 0)
+        w_scales = []
+        for o in range(3):
+            plane = keep.tile([P, PASSES, HEADS * D], U8, align_bytes=64, name="w_scales_%d" % o)
+            nc.vector.memset(plane[:].rearrange("p g n -> p (g n)").bitcast(I32), 0)
+            w_scales.append(plane)
 
         def load_x(t):
             nc.sync.dma_start(out=x_sb[:, t, :], in_=x_dram[:, t, :])
@@ -67,17 +70,31 @@ def tile_attention_pa_kernel(
                 .bitcast(I32),
             )
 
-        for t in range(TOKEN_TILES):
+        def load_scales(o):
+            for r in range(4):
+                nc.sync.dma_start(
+                    out=w_scales[o][r:P:32, :, :].bitcast(I32),
+                    in_=w_qkv_scales[:, r:16:4, HEADS * D * o : HEADS * D * (o + 1)]
+                    .rearrange("g q n -> q g n")
+                    .bitcast(I32),
+                )
+
+        def load_tables(first, last):
+            nc.sync.dma_start(out=sin_sb[:, first:last, :], in_=sin_dram[:, first:last, :])
+            nc.sync.dma_start(out=cos_sb[:, first:last, :], in_=cos_dram[:, first:last, :])
+
+        load_x(0)
+        load_tables(0, 1)
+        for t in range(1, TOKEN_TILES):
             load_x(t)
-        nc.sync.dma_start(out=sin_sb[:], in_=sin_dram)
-        nc.sync.dma_start(out=cos_sb[:], in_=cos_dram)
-        for r in range(4):
-            nc.sync.dma_start(
-                out=w_scales[r:P:32, :, :].bitcast(I32),
-                in_=w_qkv_scales[:, r:16:4, :].rearrange("g q n -> q g n").bitcast(I32),
-            )
-        for c in range(QKV // BANK):
+        load_scales(0)
+        load_words(0)
+        load_words(1)
+        load_tables(1, TOKEN_TILES)
+        for c in range(2, QKV // BANK):
             load_words(c)
+        load_scales(1)
+        load_scales(2)
 
         ident = keep.tile([P, P], F32)
         make_identity(nc, ident[:])
@@ -103,26 +120,33 @@ def tile_attention_pa_kernel(
                 out=x_codes[:, t, :].bitcast(FP8X4), scales=x_scales[:, t, :], in_=grouped[:]
             )
 
+        def lay_out_factors(t):
+            nc.scalar.copy(out=factors[:, t, 0, 0:HALF], in_=cos_sb[:, t, 0:HALF])
+            nc.scalar.mul(out=factors[:, t, 0, HALF:D], in_=sin_sb[:, t, 0:HALF], mul=-1.0)
+            nc.scalar.copy(out=factors[:, t, 1, 0:HALF], in_=sin_sb[:, t, HALF:D])
+            nc.scalar.copy(out=factors[:, t, 1, HALF:D], in_=cos_sb[:, t, HALF:D])
+
         def project(t, c):
             acc = banks.tile([P, BANK], F32, tag="bank")
+            o, b = divmod(c, BANKS_PER_OUTPUT)
             for g in range(PASSES):
                 nc.tensor.matmul_mx(
                     out=acc[:],
                     lhsT=x_codes[:, t, P * g : P * (g + 1)].bitcast(FP8X4),
                     lhsT_scale=x_scales[:, t, P * g : P * (g + 1)],
                     rhs=w_words[:, c, g, :].bitcast(FP4X4),
-                    rhs_scale=w_scales[:, g, BANK * c : BANK * (c + 1)],
+                    rhs_scale=w_scales[o][:, g, BANK * b : BANK * (b + 1)],
                     start=(g == 0),
                     stop=(g == PASSES - 1),
                 )
             return acc
 
-        for t in range(TOKEN_TILES):
+        prepare(0)
+        lay_out_factors(0)
+        for t in range(1, TOKEN_TILES):
             prepare(t)
-        nc.vector.tensor_copy(out=factors[:, :, 0, 0:HALF], in_=cos_sb[:, :, 0:HALF])
-        nc.vector.tensor_scalar_mul(out=factors[:, :, 0, HALF:D], in0=sin_sb[:, :, 0:HALF], scalar1=-1.0)
-        nc.vector.tensor_copy(out=factors[:, :, 1, 0:HALF], in_=sin_sb[:, :, HALF:D])
-        nc.vector.tensor_copy(out=factors[:, :, 1, HALF:D], in_=cos_sb[:, :, HALF:D])
+        for t in range(1, TOKEN_TILES):
+            lay_out_factors(t)
 
         def multiply(t, o):
             shape = [P, 2, HEADS_PER_BANK, D]
@@ -159,13 +183,16 @@ def tile_attention_pa_kernel(
                 nc.scalar.copy(out=v_sb[:, BANK * b : BANK * (b + 1)], in_=acc[:])
             nc.scalar.dma_start(out=v_dram[:, t, :], in_=v_sb[:])
 
-        for t in range(TOKEN_TILES - 1):
-            for o in range(2):
-                add_and_store(t, o, multiply(t, o), nc.gpsimd, 1)
-            copy_v(t)
-        last = TOKEN_TILES - 1
-        last_q = multiply(last, 0)
-        copy_v(last)
-        last_k = multiply(last, 1)
-        add_and_store(last, 0, last_q, nc.vector, 1)
-        add_and_store(last, 1, last_k, nc.vector, 2)
+        outputs = [(t, o) for o in range(2) for t in range(TOKEN_TILES)]
+        after = (3, 4, 6, 7, 9, 10, 12, 13)
+        late = []
+        for i, (t, o) in enumerate(outputs):
+            products = multiply(t, o)
+            if i < len(outputs) - 2:
+                add_and_store(t, o, products, nc.gpsimd, 1)
+            else:
+                late.append((t, o, products))
+            if i in after:
+                copy_v(after.index(i))
+        for n, (t, o, products) in enumerate(late):
+            add_and_store(t, o, products, nc.vector, n + 1)

@@ -27,6 +27,7 @@ BANK = 512
 HEADS_PER_BANK = BANK // D
 BANKS_PER_OUTPUT = HEADS // HEADS_PER_BANK
 
+TENSOR_SUM = 10
 FLOPS = 2 * TOKENS * HID * QKV
 
 
@@ -148,9 +149,8 @@ def tile_attention_pa_kernel(
         for t in range(1, TOKEN_TILES):
             lay_out_factors(t)
 
-        def multiply(t, o):
+        def multiply(t, o, products):
             shape = [P, 2, HEADS_PER_BANK, D]
-            products = results.tile([P, 2, HEADS, D], F32)
             for b in range(BANKS_PER_OUTPUT):
                 acc = project(t, BANKS_PER_OUTPUT * o + b)
                 nc.vector.tensor_tensor(
@@ -159,22 +159,35 @@ def tile_attention_pa_kernel(
                     in1=factors[:, t, :, :].unsqueeze(2).to_broadcast(shape),
                     op=ALU.mult,
                 )
-            return products
 
-        def add_and_store(t, o, products, adder, pieces):
-            rotated = results.tile([P, HEADS, D], F32)
-            step = HEADS // pieces
-            for h in range(0, HEADS, step):
-                adder.tensor_tensor(
-                    out=rotated[:, h : h + step, :].rearrange("p h (r j) -> p r h j", r=2),
-                    in0=products[:, :, h : h + step, 0:HALF],
-                    in1=products[:, :, h : h + step, HALF:D],
-                    op=ALU.add,
+        def add_and_store(t, o, products, rotated, adder, first, last):
+            adder.tensor_tensor(
+                out=rotated[:, first:last, :].rearrange("p h (r j) -> p r h j", r=2),
+                in0=products[:, :, first:last, 0:HALF],
+                in1=products[:, :, first:last, HALF:D],
+                op=ALU.add,
+            )
+            nc.sync.dma_start(
+                out=rotated_dram[o][:, t, D * first : D * last],
+                in_=rotated[:, first:last, :].rearrange("p h d -> p (h d)"),
+            )
+
+        def add_on_tensor(t, o, products, rotated, b):
+            first, last = HEADS_PER_BANK * b, HEADS_PER_BANK * (b + 1)
+            total = banks.tile([P, BANK], F32, tag="bank")
+            for e in range(2):
+                nc.tensor.matmul(
+                    out=total[:].rearrange("p (h r j) -> p h r j", r=2, j=HALF),
+                    lhsT=ident[:],
+                    rhs=products[:, :, first:last, HALF * e : HALF * (e + 1)].rearrange("p r h j -> p h r j"),
+                    start=(e == 0),
+                    stop=(e == 1),
                 )
-                nc.sync.dma_start(
-                    out=rotated_dram[o][:, t, D * h : D * (h + step)],
-                    in_=rotated[:, h : h + step, :].rearrange("p h d -> p (h d)"),
-                )
+            nc.scalar.copy(out=rotated[:, first:last, :].rearrange("p h d -> p (h d)"), in_=total[:])
+            nc.sync.dma_start(
+                out=rotated_dram[o][:, t, D * first : D * last],
+                in_=rotated[:, first:last, :].rearrange("p h d -> p (h d)"),
+            )
 
         def copy_v(t):
             v_sb = results.tile([P, HEADS * D], F32)
@@ -187,12 +200,26 @@ def tile_attention_pa_kernel(
         after = (3, 4, 6, 7, 9, 10, 12, 13)
         late = []
         for i, (t, o) in enumerate(outputs):
-            products = multiply(t, o)
-            if i < len(outputs) - 2:
-                add_and_store(t, o, products, nc.gpsimd, 1)
+            if i == TENSOR_SUM:
+                products = keep.tile([P, 2, HEADS, D], F32, name="held_products")
+                rotated = keep.tile([P, HEADS, D], F32, name="held_rotated")
+                held = (t, o, products, rotated)
             else:
-                late.append((t, o, products))
+                products = results.tile([P, 2, HEADS, D], F32, tag="products")
+                rotated = results.tile([P, HEADS, D], F32, tag="rotated")
+            multiply(t, o, products)
+            if i == TENSOR_SUM + 3:
+                add_on_tensor(held[0], held[1], held[2], held[3], 0)
+            if i == TENSOR_SUM + 5:
+                add_on_tensor(held[0], held[1], held[2], held[3], 1)
+            if i == TENSOR_SUM:
+                pass
+            elif i < len(outputs) - 1:
+                add_and_store(t, o, products, rotated, nc.gpsimd, 0, HEADS)
+            else:
+                late.append((t, o, products, rotated, 0))
+                late.append((t, o, products, rotated, HEADS_PER_BANK))
             if i in after:
                 copy_v(after.index(i))
-        for n, (t, o, products) in enumerate(late):
-            add_and_store(t, o, products, nc.vector, n + 1)
+        for t, o, products, rotated, first in late:
+            add_and_store(t, o, products, rotated, nc.vector, first, first + HEADS_PER_BANK)

@@ -142,23 +142,26 @@ def tile_attention_pa_kernel(
                 )
             return acc
 
+        def multiply(t, o, products, b):
+            shape = [P, 2, HEADS_PER_BANK, D]
+            acc = project(t, BANKS_PER_OUTPUT * o + b)
+            nc.vector.tensor_tensor(
+                out=products[:, :, HEADS_PER_BANK * b : HEADS_PER_BANK * (b + 1), :],
+                in0=acc[:].rearrange("p (h d) -> p h d", d=D).unsqueeze(1).to_broadcast(shape),
+                in1=factors[:, t, :, :].unsqueeze(2).to_broadcast(shape),
+                op=ALU.mult,
+            )
+
         prepare(0)
         lay_out_factors(0)
-        for t in range(1, TOKEN_TILES):
+        for t in range(1, TOKEN_TILES - 1):
             prepare(t)
+        first_products = results.tile([P, 2, HEADS, D], F32, tag="products")
+        multiply(0, 0, first_products, 0)
+        prepare(TOKEN_TILES - 1)
         for t in range(1, TOKEN_TILES):
             lay_out_factors(t)
 
-        def multiply(t, o, products):
-            shape = [P, 2, HEADS_PER_BANK, D]
-            for b in range(BANKS_PER_OUTPUT):
-                acc = project(t, BANKS_PER_OUTPUT * o + b)
-                nc.vector.tensor_tensor(
-                    out=products[:, :, HEADS_PER_BANK * b : HEADS_PER_BANK * (b + 1), :],
-                    in0=acc[:].rearrange("p (h d) -> p h d", d=D).unsqueeze(1).to_broadcast(shape),
-                    in1=factors[:, t, :, :].unsqueeze(2).to_broadcast(shape),
-                    op=ALU.mult,
-                )
 
         def add_and_store(t, o, products, rotated, adder, first, last):
             adder.tensor_tensor(
@@ -204,18 +207,26 @@ def tile_attention_pa_kernel(
                 products = keep.tile([P, 2, HEADS, D], F32, name="held_products")
                 rotated = keep.tile([P, HEADS, D], F32, name="held_rotated")
                 held = (t, o, products, rotated)
+            elif i == 0:
+                products = first_products
+                rotated = results.tile([P, HEADS, D], F32, tag="rotated")
             else:
                 products = results.tile([P, 2, HEADS, D], F32, tag="products")
                 rotated = results.tile([P, HEADS, D], F32, tag="rotated")
-            multiply(t, o, products)
+            if i > 0:
+                multiply(t, o, products, 0)
+            multiply(t, o, products, 1)
             if i == TENSOR_SUM + 3:
                 add_on_tensor(held[0], held[1], held[2], held[3], 0)
             if i == TENSOR_SUM + 5:
                 add_on_tensor(held[0], held[1], held[2], held[3], 1)
             if i == TENSOR_SUM:
                 pass
-            elif i < len(outputs) - 1:
+            elif i < len(outputs) - 2:
                 add_and_store(t, o, products, rotated, nc.gpsimd, 0, HEADS)
+            elif i == len(outputs) - 2:
+                add_and_store(t, o, products, rotated, nc.gpsimd, 0, HEADS_PER_BANK)
+                add_and_store(t, o, products, rotated, nc.gpsimd, HEADS_PER_BANK, HEADS)
             else:
                 late.append((t, o, products, rotated, 0))
                 late.append((t, o, products, rotated, HEADS_PER_BANK))

@@ -86,9 +86,11 @@ def tile_attention_pa_kernel(
 
         load_x(0)
         load_tables(0, 1)
-        for t in range(1, TOKEN_TILES):
+        for t in range(1, TOKEN_TILES // 2):
             load_x(t)
         load_scales(0)
+        for t in range(TOKEN_TILES // 2, TOKEN_TILES):
+            load_x(t)
         load_words(0)
         load_words(1)
         load_tables(1, TOKEN_TILES)

@@ -27,7 +27,8 @@ BANK = 512
 HEADS_PER_BANK = BANK // D
 BANKS_PER_OUTPUT = HEADS // HEADS_PER_BANK
 
-TENSOR_SUM = 10
+TURNED = (6, 10, 14)
+TURN_LAG = 4
 FLOPS = 2 * TOKENS * HID * QKV
 
 
@@ -85,22 +86,29 @@ def tile_attention_pa_kernel(
             nc.sync.dma_start(out=cos_sb[:, first:last, :], in_=cos_dram[:, first:last, :])
 
         load_x(0)
-        load_tables(0, 1)
-        for t in range(1, TOKEN_TILES // 2):
+        load_tables(0, 2)
+        for t in range(1, 5):
             load_x(t)
         load_scales(0)
-        for t in range(TOKEN_TILES // 2, TOKEN_TILES):
-            load_x(t)
         load_words(0)
+        for t in range(5, TOKEN_TILES):
+            load_x(t)
         load_words(1)
-        load_tables(1, TOKEN_TILES)
-        for c in range(2, QKV // BANK):
-            load_words(c)
-        load_scales(1)
+        load_tables(2, TOKEN_TILES)
+        load_words(4)
+        load_words(5)
         load_scales(2)
+        load_scales(1)
+        load_words(2)
+        load_words(3)
 
         ident = keep.tile([P, P], F32)
         make_identity(nc, ident[:])
+        ident_bf16 = keep.tile([P, P], BF16)
+        nc.scalar.copy(out=ident_bf16[:], in_=ident[:])
+        swap = keep.tile([P, P], F32)
+        nc.scalar.copy(out=swap[:, 0:HALF], in_=ident[:, HALF:D])
+        nc.scalar.copy(out=swap[:, HALF:D], in_=ident[:, 0:HALF])
 
         x_codes = keep.tile([P, TOKEN_TILES, PASSES * P], U32, align_bytes=64)
         x_scales = keep.tile([P, TOKEN_TILES, PASSES * P], U8, align_bytes=64)
@@ -123,11 +131,12 @@ def tile_attention_pa_kernel(
                 out=x_codes[:, t, :].bitcast(FP8X4), scales=x_scales[:, t, :], in_=grouped[:]
             )
 
-        def lay_out_factors(t):
-            nc.scalar.copy(out=factors[:, t, 0, 0:HALF], in_=cos_sb[:, t, 0:HALF])
-            nc.scalar.mul(out=factors[:, t, 0, HALF:D], in_=sin_sb[:, t, 0:HALF], mul=-1.0)
-            nc.scalar.copy(out=factors[:, t, 1, 0:HALF], in_=sin_sb[:, t, HALF:D])
-            nc.scalar.copy(out=factors[:, t, 1, HALF:D], in_=cos_sb[:, t, HALF:D])
+        def lay_out_factors(copy, multiply_by, first, last):
+            tiles = slice(first, last)
+            copy(out=factors[:, tiles, 0, 0:HALF], in_=cos_sb[:, tiles, 0:HALF])
+            multiply_by(factors[:, tiles, 0, HALF:D], sin_sb[:, tiles, 0:HALF], -1.0)
+            copy(out=factors[:, tiles, 1, 0:HALF], in_=sin_sb[:, tiles, HALF:D])
+            copy(out=factors[:, tiles, 1, HALF:D], in_=cos_sb[:, tiles, HALF:D])
 
         def project(t, c):
             acc = banks.tile([P, BANK], F32, tag="bank")
@@ -144,6 +153,61 @@ def tile_attention_pa_kernel(
                 )
             return acc
 
+        crossed = {}
+        turned_tables = {}
+
+        def cross_sines(t):
+            row = keep.tile([P, D], BF16, name="crossed_%d" % t)
+            nc.scalar.copy(out=row[:, 0:HALF], in_=sin_sb[:, t, HALF:D])
+            nc.scalar.mul(out=row[:, HALF:D], in_=sin_sb[:, t, 0:HALF], mul=-1.0)
+            crossed[t] = row
+
+        def turn_tables(t):
+            turned = banks.tile([P, 2, P], BF16, tag="bank")
+            nc.tensor.transpose(turned[:, 0, :], cos_sb[:, t, :], ident_bf16[:])
+            nc.tensor.transpose(turned[:, 1, :], crossed[t][:], ident_bf16[:])
+            table = keep.tile([P, 2, P], BF16, name="turned_table_%d" % t)
+            nc.scalar.copy(out=table[:], in_=turned[:])
+            turned_tables[t] = table
+
+        def turned_products(t, o, b):
+            acc = banks.tile([P, HEADS_PER_BANK, P], F32, tag="bank")
+            c = BANKS_PER_OUTPUT * o + b
+            for h in range(HEADS_PER_BANK):
+                for g in range(PASSES):
+                    nc.tensor.matmul_mx(
+                        out=acc[:, h, :],
+                        lhsT=w_words[:, c, g, 2 * D * h : 2 * D * (h + 1)].bitcast(FP4X4),
+                        lhsT_scale=w_scales[o][:, g, BANK * b + D * h : BANK * b + D * (h + 1)],
+                        rhs=x_codes[:, t, P * g : P * (g + 1)].bitcast(FP8X4),
+                        rhs_scale=x_scales[:, t, P * g : P * (g + 1)],
+                        start=(g == 0),
+                        stop=(g == PASSES - 1),
+                    )
+            shape = [P, 2, HEADS_PER_BANK, P]
+            products = results.tile([P, 2, HEADS_PER_BANK, P], F32, tag="turned_products")
+            nc.vector.tensor_tensor(
+                out=products[:],
+                in0=acc[:].unsqueeze(1).to_broadcast(shape),
+                in1=turned_tables[t][:].unsqueeze(2).to_broadcast(shape),
+                op=ALU.mult,
+            )
+            return products
+
+        def turn_back(t, o, b, products, rotated):
+            total = banks.tile([P, HEADS_PER_BANK, D], F32, tag="bank")
+            for h in range(HEADS_PER_BANK):
+                nc.tensor.matmul(out=total[:, h, :], lhsT=products[:, 0, h, :], rhs=ident[:],
+                                 start=True, stop=False, is_transpose=True)
+                nc.tensor.matmul(out=total[:, h, :], lhsT=products[:, 1, h, :], rhs=swap[:],
+                                 start=False, stop=True, is_transpose=True)
+            first, last = HEADS_PER_BANK * b, HEADS_PER_BANK * (b + 1)
+            nc.scalar.copy(out=rotated[:, first:last, :], in_=total[:])
+            if b == BANKS_PER_OUTPUT - 1:
+                nc.scalar.dma_start(
+                    out=rotated_dram[o][:, t, :], in_=rotated[:].rearrange("p h d -> p (h d)")
+                )
+
         def multiply(t, o, products, b):
             shape = [P, 2, HEADS_PER_BANK, D]
             acc = project(t, BANKS_PER_OUTPUT * o + b)
@@ -153,17 +217,6 @@ def tile_attention_pa_kernel(
                 in1=factors[:, t, :, :].unsqueeze(2).to_broadcast(shape),
                 op=ALU.mult,
             )
-
-        prepare(0)
-        lay_out_factors(0)
-        for t in range(1, TOKEN_TILES - 1):
-            prepare(t)
-        first_products = results.tile([P, 2, HEADS, D], F32, tag="products")
-        multiply(0, 0, first_products, 0)
-        prepare(TOKEN_TILES - 1)
-        for t in range(1, TOKEN_TILES):
-            lay_out_factors(t)
-
 
         def add_and_store(t, o, products, rotated, adder, first, last):
             adder.tensor_tensor(
@@ -177,23 +230,6 @@ def tile_attention_pa_kernel(
                 in_=rotated[:, first:last, :].rearrange("p h d -> p (h d)"),
             )
 
-        def add_on_tensor(t, o, products, rotated, b):
-            first, last = HEADS_PER_BANK * b, HEADS_PER_BANK * (b + 1)
-            total = banks.tile([P, BANK], F32, tag="bank")
-            for e in range(2):
-                nc.tensor.matmul(
-                    out=total[:].rearrange("p (h r j) -> p h r j", r=2, j=HALF),
-                    lhsT=ident[:],
-                    rhs=products[:, :, first:last, HALF * e : HALF * (e + 1)].rearrange("p r h j -> p h r j"),
-                    start=(e == 0),
-                    stop=(e == 1),
-                )
-            nc.scalar.copy(out=rotated[:, first:last, :].rearrange("p h d -> p (h d)"), in_=total[:])
-            nc.sync.dma_start(
-                out=rotated_dram[o][:, t, D * first : D * last],
-                in_=rotated[:, first:last, :].rearrange("p h d -> p (h d)"),
-            )
-
         def copy_v(t):
             v_sb = results.tile([P, HEADS * D], F32)
             for b in range(BANKS_PER_OUTPUT):
@@ -201,38 +237,57 @@ def tile_attention_pa_kernel(
                 nc.scalar.copy(out=v_sb[:, BANK * b : BANK * (b + 1)], in_=acc[:])
             nc.scalar.dma_start(out=v_dram[:, t, :], in_=v_sb[:])
 
+        waiting = []
+
+        def bank_done():
+            for entry in waiting:
+                entry[0] -= 1
+            while waiting and waiting[0][0] < 0:
+                turn_back(*waiting.pop(0)[1])
+
+        def start_turned(t, o, b, rotated):
+            products = turned_products(t, o, b)
+            outputs_left = len(outputs) - 1 - (TOKEN_TILES * o + t)
+            waiting.append([min(TURN_LAG, BANKS_PER_OUTPUT * outputs_left), (t, o, b, products, rotated)])
+            bank_done()
+
         outputs = [(t, o) for o in range(2) for t in range(TOKEN_TILES)]
         after = (3, 4, 6, 7, 9, 10, 12, 13)
-        late = []
-        for i, (t, o) in enumerate(outputs):
-            if i == TENSOR_SUM:
-                products = keep.tile([P, 2, HEADS, D], F32, name="held_products")
-                rotated = keep.tile([P, HEADS, D], F32, name="held_rotated")
-                held = (t, o, products, rotated)
-            elif i == 0:
-                products = first_products
-                rotated = results.tile([P, HEADS, D], F32, tag="rotated")
-            else:
-                products = results.tile([P, 2, HEADS, D], F32, tag="products")
-                rotated = results.tile([P, HEADS, D], F32, tag="rotated")
-            if i > 0:
-                multiply(t, o, products, 0)
-            multiply(t, o, products, 1)
-            if i == TENSOR_SUM + 3:
-                add_on_tensor(held[0], held[1], held[2], held[3], 0)
-            if i == TENSOR_SUM + 5:
-                add_on_tensor(held[0], held[1], held[2], held[3], 1)
-            if i == TENSOR_SUM:
-                pass
-            elif i < len(outputs) - 2:
-                add_and_store(t, o, products, rotated, nc.gpsimd, 0, HEADS)
-            elif i == len(outputs) - 2:
-                add_and_store(t, o, products, rotated, nc.gpsimd, 0, HEADS_PER_BANK)
-                add_and_store(t, o, products, rotated, nc.gpsimd, HEADS_PER_BANK, HEADS)
-            else:
-                late.append((t, o, products, rotated, 0))
-                late.append((t, o, products, rotated, HEADS_PER_BANK))
-            if i in after:
-                copy_v(after.index(i))
-        for t, o, products, rotated, first in late:
-            add_and_store(t, o, products, rotated, nc.vector, first, first + HEADS_PER_BANK)
+        with tc.manual_schedule():
+            prepare(0)
+            lay_out_factors(nc.vector.tensor_copy, nc.vector.tensor_scalar_mul, 0, 2)
+            for t in range(1, 5):
+                prepare(t)
+            products = {}
+            for i in range(2):
+                products[i] = results.tile([P, 2, HEADS, D], F32, name="products_%d" % i, tag="products")
+                multiply(i, 0, products[i], 0)
+            for t in range(5, TOKEN_TILES):
+                prepare(t)
+            lay_out_factors(nc.scalar.copy, nc.scalar.mul, 2, 4)
+            lay_out_factors(nc.scalar.copy, nc.scalar.mul, 4, TOKEN_TILES)
+            for t in sorted({outputs[i][0] for i in TURNED}):
+                cross_sines(t)
+            for i, (t, o) in enumerate(outputs):
+                if i + 1 in TURNED and outputs[i + 1][0] not in turned_tables:
+                    turn_tables(outputs[i + 1][0])
+                if i in TURNED:
+                    rotated = results.tile([P, HEADS, D], F32, tag="turned")
+                    for b in range(BANKS_PER_OUTPUT):
+                        start_turned(t, o, b, rotated)
+                else:
+                    rotated = results.tile([P, HEADS, D], F32, tag="rotated")
+                    if i not in products:
+                        products[i] = results.tile([P, 2, HEADS, D], F32, name="products_%d" % i, tag="products")
+                        multiply(t, o, products[i], 0)
+                        bank_done()
+                    if i == len(outputs) - 1:
+                        add_and_store(t, o, products[i], rotated, nc.gpsimd, 0, HEADS_PER_BANK)
+                    multiply(t, o, products[i], 1)
+                    bank_done()
+                    if i < len(outputs) - 1:
+                        add_and_store(t, o, products[i], rotated, nc.gpsimd, 0, HEADS)
+                    else:
+                        add_and_store(t, o, products[i], rotated, nc.vector, HEADS_PER_BANK, HEADS)
+                if i in after:
+                    copy_v(after.index(i))

@@ -54,31 +54,40 @@ def tile_attention_pa_kernel(
         x_sb = keep.tile([P, TOKEN_TILES, HID], BF16)
         cos_sb = keep.tile([P, TOKEN_TILES, D], BF16)
         sin_sb = keep.tile([P, TOKEN_TILES, D], BF16)
-        w_words = keep.tile([P, QKV // BANK, PASSES, 2 * BANK], U8, align_bytes=64)
+        w_pieces = []
+        for first, count in ((0, 1), (1, 1), (2, 2), (4, 2)):
+            words = keep.tile([P, PASSES, 2 * BANK * count], U8, align_bytes=64, name="w_words_%d" % first)
+            w_pieces.append((first, count, words))
+        w_words = {first + b: (words, b) for first, count, words in w_pieces for b in range(count)}
         w_scales = []
-        for o in range(3):
-            plane = keep.tile([P, PASSES, HEADS * D], U8, align_bytes=64, name="w_scales_%d" % o)
+        for outputs_in in (1, 2):
+            plane = keep.tile([P, PASSES, HEADS * D * outputs_in], U8, align_bytes=64, name="w_scales_%d" % outputs_in)
             nc.vector.memset(plane[:].rearrange("p g n -> p (g n)").bitcast(I32), 0)
             w_scales.append(plane)
+
+        def scale_columns(c, first, last):
+            if c < BANKS_PER_OUTPUT:
+                return w_scales[0], slice(BANK * c + first, BANK * c + last)
+            return w_scales[1], slice(BANK * (c - BANKS_PER_OUTPUT) + first, BANK * (c - BANKS_PER_OUTPUT) + last)
 
         def load_x(t):
             nc.sync.dma_start(out=x_sb[:, t, :], in_=x_dram[:, t, :])
 
-        def load_words(c):
+        def load_words(piece):
+            first, count, words = w_pieces[piece]
             nc.sync.dma_start(
-                out=w_words[:, c, :, :].bitcast(I32),
-                in_=w_qkv_words[:, :, 2 * BANK * c : 2 * BANK * (c + 1)]
+                out=words[:].bitcast(I32),
+                in_=w_qkv_words[:, :, 2 * BANK * first : 2 * BANK * (first + count)]
                 .rearrange("g p n -> p g n")
                 .bitcast(I32),
             )
 
-        def load_scales(o):
+        def load_scales(tile):
+            first, last = ((0, HEADS * D), (HEADS * D, QKV))[tile]
             for r in range(4):
                 nc.sync.dma_start(
-                    out=w_scales[o][r:P:32, :, :].bitcast(I32),
-                    in_=w_qkv_scales[:, r:16:4, HEADS * D * o : HEADS * D * (o + 1)]
-                    .rearrange("g q n -> q g n")
-                    .bitcast(I32),
+                    out=w_scales[tile][r:P:32, :, :].bitcast(I32),
+                    in_=w_qkv_scales[:, r:16:4, first:last].rearrange("g q n -> q g n").bitcast(I32),
                 )
 
         def load_tables(first, last):
@@ -95,12 +104,9 @@ def tile_attention_pa_kernel(
             load_x(t)
         load_words(1)
         load_tables(2, TOKEN_TILES)
-        load_words(4)
-        load_words(5)
-        load_scales(2)
+        load_words(3)
         load_scales(1)
         load_words(2)
-        load_words(3)
 
         ident = keep.tile([P, P], F32)
         make_identity(nc, ident[:])
@@ -140,14 +146,15 @@ def tile_attention_pa_kernel(
 
         def project(t, c):
             acc = banks.tile([P, BANK], F32, tag="bank")
-            o, b = divmod(c, BANKS_PER_OUTPUT)
+            words, at = w_words[c]
+            scales, columns = scale_columns(c, 0, BANK)
             for g in range(PASSES):
                 nc.tensor.matmul_mx(
                     out=acc[:],
                     lhsT=x_codes[:, t, P * g : P * (g + 1)].bitcast(FP8X4),
                     lhsT_scale=x_scales[:, t, P * g : P * (g + 1)],
-                    rhs=w_words[:, c, g, :].bitcast(FP4X4),
-                    rhs_scale=w_scales[o][:, g, BANK * b : BANK * (b + 1)],
+                    rhs=words[:, g, 2 * BANK * at : 2 * BANK * (at + 1)].bitcast(FP4X4),
+                    rhs_scale=scales[:, g, columns],
                     start=(g == 0),
                     stop=(g == PASSES - 1),
                 )
@@ -172,13 +179,14 @@ def tile_attention_pa_kernel(
 
         def turned_products(t, o, b):
             acc = banks.tile([P, HEADS_PER_BANK, P], F32, tag="bank")
-            c = BANKS_PER_OUTPUT * o + b
+            words, at = w_words[BANKS_PER_OUTPUT * o + b]
             for h in range(HEADS_PER_BANK):
+                scales, columns = scale_columns(BANKS_PER_OUTPUT * o + b, D * h, D * (h + 1))
                 for g in range(PASSES):
                     nc.tensor.matmul_mx(
                         out=acc[:, h, :],
-                        lhsT=w_words[:, c, g, 2 * D * h : 2 * D * (h + 1)].bitcast(FP4X4),
-                        lhsT_scale=w_scales[o][:, g, BANK * b + D * h : BANK * b + D * (h + 1)],
+                        lhsT=words[:, g, 2 * (BANK * at + D * h) : 2 * (BANK * at + D * (h + 1))].bitcast(FP4X4),
+                        lhsT_scale=scales[:, g, columns],
                         rhs=x_codes[:, t, P * g : P * (g + 1)].bitcast(FP8X4),
                         rhs_scale=x_scales[:, t, P * g : P * (g + 1)],
                         start=(g == 0),
@@ -230,12 +238,17 @@ def tile_attention_pa_kernel(
                 in_=rotated[:, first:last, :].rearrange("p h d -> p (h d)"),
             )
 
+        v_pair = []
+
         def copy_v(t):
-            v_sb = results.tile([P, HEADS * D], F32)
+            if t % 2 == 0:
+                v_pair.append(results.tile([P, 2, HEADS * D], F32, name="v_%d" % t, tag="v"))
+            v_sb = v_pair[-1]
             for b in range(BANKS_PER_OUTPUT):
                 acc = project(t, BANKS_PER_OUTPUT * 2 + b)
-                nc.scalar.copy(out=v_sb[:, BANK * b : BANK * (b + 1)], in_=acc[:])
-            nc.scalar.dma_start(out=v_dram[:, t, :], in_=v_sb[:])
+                nc.scalar.copy(out=v_sb[:, t % 2, BANK * b : BANK * (b + 1)], in_=acc[:])
+            if t % 2 == 1:
+                nc.scalar.dma_start(out=v_dram[:, t - 1 : t + 1, :], in_=v_sb[:])
 
         waiting = []
 

@@ -27,8 +27,10 @@ BANK = 512
 HEADS_PER_BANK = BANK // D
 BANKS_PER_OUTPUT = HEADS // HEADS_PER_BANK
 
-TURNED = (6, 10, 14)
-TURN_LAG = 4
+TURNED = {10: (0, 1), 12: (0, 1), 14: (0,), 15: (0,)}
+SHARED = ()
+TURN_LAG = 3
+SHARED_LAG = 11
 FLOPS = 2 * TOKENS * HID * QKV
 
 
@@ -103,9 +105,9 @@ def tile_attention_pa_kernel(
         for t in range(5, TOKEN_TILES):
             load_x(t)
         load_words(1)
-        load_tables(2, TOKEN_TILES)
-        load_words(3)
         load_scales(1)
+        load_words(3)
+        load_tables(2, TOKEN_TILES)
         load_words(2)
 
         ident = keep.tile([P, P], F32)
@@ -177,7 +179,7 @@ def tile_attention_pa_kernel(
             nc.scalar.copy(out=table[:], in_=turned[:])
             turned_tables[t] = table
 
-        def turned_products(t, o, b):
+        def turned_products(t, o, b, shared):
             acc = banks.tile([P, HEADS_PER_BANK, P], F32, tag="bank")
             words, at = w_words[BANKS_PER_OUTPUT * o + b]
             for h in range(HEADS_PER_BANK):
@@ -192,17 +194,28 @@ def tile_attention_pa_kernel(
                         start=(g == 0),
                         stop=(g == PASSES - 1),
                     )
-            shape = [P, 2, HEADS_PER_BANK, P]
             products = results.tile([P, 2, HEADS_PER_BANK, P], F32, tag="turned_products")
-            nc.vector.tensor_tensor(
-                out=products[:],
-                in0=acc[:].unsqueeze(1).to_broadcast(shape),
-                in1=turned_tables[t][:].unsqueeze(2).to_broadcast(shape),
-                op=ALU.mult,
-            )
+            if shared:
+                u = results.tile([P, HEADS_PER_BANK, P], F32)
+                nc.scalar.copy(out=u[:], in_=acc[:])
+                for engine, source, r in ((nc.vector, acc, 0), (nc.gpsimd, u, 1)):
+                    engine.tensor_tensor(
+                        out=products[:, r, :, :],
+                        in0=source[:],
+                        in1=turned_tables[t][:, r, :].unsqueeze(1).to_broadcast([P, HEADS_PER_BANK, P]),
+                        op=ALU.mult,
+                    )
+            else:
+                shape = [P, 2, HEADS_PER_BANK, P]
+                nc.vector.tensor_tensor(
+                    out=products[:],
+                    in0=acc[:].unsqueeze(1).to_broadcast(shape),
+                    in1=turned_tables[t][:].unsqueeze(2).to_broadcast(shape),
+                    op=ALU.mult,
+                )
             return products
 
-        def turn_back(t, o, b, products, rotated):
+        def turn_back(t, o, b, products, rotated, stored):
             total = banks.tile([P, HEADS_PER_BANK, D], F32, tag="bank")
             for h in range(HEADS_PER_BANK):
                 nc.tensor.matmul(out=total[:, h, :], lhsT=products[:, 0, h, :], rhs=ident[:],
@@ -211,9 +224,10 @@ def tile_attention_pa_kernel(
                                  start=False, stop=True, is_transpose=True)
             first, last = HEADS_PER_BANK * b, HEADS_PER_BANK * (b + 1)
             nc.scalar.copy(out=rotated[:, first:last, :], in_=total[:])
-            if b == BANKS_PER_OUTPUT - 1:
+            if stored:
                 nc.scalar.dma_start(
-                    out=rotated_dram[o][:, t, :], in_=rotated[:].rearrange("p h d -> p (h d)")
+                    out=rotated_dram[o][:, t, D * stored[0] : D * stored[1]],
+                    in_=rotated[:, stored[0] : stored[1], :].rearrange("p h d -> p (h d)"),
                 )
 
         def multiply(t, o, products, b):
@@ -255,52 +269,59 @@ def tile_attention_pa_kernel(
         def bank_done():
             for entry in waiting:
                 entry[0] -= 1
-            while waiting and waiting[0][0] < 0:
-                turn_back(*waiting.pop(0)[1])
+            for entry in [e for e in waiting if e[0] < 0]:
+                waiting.remove(entry)
+                turn_back(*entry[1])
 
-        def start_turned(t, o, b, rotated):
-            products = turned_products(t, o, b)
-            outputs_left = len(outputs) - 1 - (TOKEN_TILES * o + t)
-            waiting.append([min(TURN_LAG, BANKS_PER_OUTPUT * outputs_left), (t, o, b, products, rotated)])
+        def start_turned(i, b, rotated, stored):
+            t, o = outputs[i]
+            shared = (i, b) in SHARED
+            products = turned_products(t, o, b, shared)
+            following = BANKS_PER_OUTPUT * (len(outputs) - i) - 1 - b
+            lag = min(SHARED_LAG if shared else TURN_LAG, following)
+            waiting.append([lag, (t, o, b, products, rotated, stored)])
             bank_done()
 
         outputs = [(t, o) for o in range(2) for t in range(TOKEN_TILES)]
-        after = (3, 4, 6, 7, 9, 10, 12, 13)
         with tc.manual_schedule():
             prepare(0)
             lay_out_factors(nc.vector.tensor_copy, nc.vector.tensor_scalar_mul, 0, 2)
             for t in range(1, 5):
                 prepare(t)
-            products = {}
+            started = {}
             for i in range(2):
-                products[i] = results.tile([P, 2, HEADS, D], F32, name="products_%d" % i, tag="products")
-                multiply(i, 0, products[i], 0)
+                started[i] = results.tile([P, 2, HEADS, D], F32, name="products_%d" % i, tag="products")
+                multiply(i, 0, started[i], 0)
             for t in range(5, TOKEN_TILES):
                 prepare(t)
             lay_out_factors(nc.scalar.copy, nc.scalar.mul, 2, 4)
             lay_out_factors(nc.scalar.copy, nc.scalar.mul, 4, TOKEN_TILES)
             for t in sorted({outputs[i][0] for i in TURNED}):
                 cross_sines(t)
+            last = len(outputs) - 1
             for i, (t, o) in enumerate(outputs):
                 if i + 1 in TURNED and outputs[i + 1][0] not in turned_tables:
                     turn_tables(outputs[i + 1][0])
-                if i in TURNED:
-                    rotated = results.tile([P, HEADS, D], F32, tag="turned")
-                    for b in range(BANKS_PER_OUTPUT):
-                        start_turned(t, o, b, rotated)
-                else:
-                    rotated = results.tile([P, HEADS, D], F32, tag="rotated")
-                    if i not in products:
-                        products[i] = results.tile([P, 2, HEADS, D], F32, name="products_%d" % i, tag="products")
-                        multiply(t, o, products[i], 0)
+                turned = TURNED.get(i, ())
+                rotated = results.tile([P, HEADS, D], F32, tag="turned" if turned else "rotated")
+                if i in started:
+                    products = started[i]
+                elif len(turned) < BANKS_PER_OUTPUT:
+                    products = results.tile([P, 2, HEADS, D], F32, tag="products")
+                by_bank = len(turned) == 1 or i == last - 1
+                for b in range(BANKS_PER_OUTPUT):
+                    heads = (HEADS_PER_BANK * b, HEADS_PER_BANK * (b + 1))
+                    if b in turned:
+                        whole = len(turned) == BANKS_PER_OUTPUT
+                        stored = heads if not whole else (0, HEADS) if b == BANKS_PER_OUTPUT - 1 else None
+                        start_turned(i, b, rotated, stored)
+                        continue
+                    if b > 0 or i not in started:
+                        multiply(t, o, products, b)
                         bank_done()
-                    if i == len(outputs) - 1:
-                        add_and_store(t, o, products[i], rotated, nc.gpsimd, 0, HEADS_PER_BANK)
-                    multiply(t, o, products[i], 1)
-                    bank_done()
-                    if i < len(outputs) - 1:
-                        add_and_store(t, o, products[i], rotated, nc.gpsimd, 0, HEADS)
-                    else:
-                        add_and_store(t, o, products[i], rotated, nc.vector, HEADS_PER_BANK, HEADS)
-                if i in after:
-                    copy_v(after.index(i))
+                    if by_bank:
+                        add_and_store(t, o, products, rotated, nc.vector if i == last else nc.gpsimd, *heads)
+                if not turned and not by_bank:
+                    add_and_store(t, o, products, rotated, nc.gpsimd, 0, HEADS)
+                if 1 <= i <= TOKEN_TILES:
+                    copy_v(i - 1)

@@ -105,9 +105,9 @@ def tile_attention_pa_kernel(
         for t in range(5, TOKEN_TILES):
             load_x(t)
         load_words(1)
+        load_tables(2, TOKEN_TILES)
         load_scales(1)
         load_words(3)
-        load_tables(2, TOKEN_TILES)
         load_words(2)
 
         ident = keep.tile([P, P], F32)
@@ -294,8 +294,8 @@ def tile_attention_pa_kernel(
                 multiply(i, 0, started[i], 0)
             for t in range(5, TOKEN_TILES):
                 prepare(t)
-            lay_out_factors(nc.scalar.copy, nc.scalar.mul, 2, 4)
-            lay_out_factors(nc.scalar.copy, nc.scalar.mul, 4, TOKEN_TILES)
+            lay_out_factors(nc.scalar.copy, nc.scalar.mul, 2, 3)
+            lay_out_factors(nc.scalar.copy, nc.scalar.mul, 3, TOKEN_TILES)
             for t in sorted({outputs[i][0] for i in TURNED}):
                 cross_sines(t)
             last = len(outputs) - 1
@@ -323,5 +323,5 @@ def tile_attention_pa_kernel(
                         add_and_store(t, o, products, rotated, nc.vector if i == last else nc.gpsimd, *heads)
                 if not turned and not by_bank:
                     add_and_store(t, o, products, rotated, nc.gpsimd, 0, HEADS)
-                if 1 <= i <= TOKEN_TILES:
-                    copy_v(i - 1)
+                if 2 <= i < TOKEN_TILES + 2:
+                    copy_v(i - 2)

@@ -171,13 +171,15 @@ def tile_attention_pa_kernel(
             nc.scalar.mul(out=row[:, HALF:D], in_=sin_sb[:, t, 0:HALF], mul=-1.0)
             crossed[t] = row
 
-        def turn_tables(t):
-            turned = banks.tile([P, 2, P], BF16, tag="bank")
-            nc.tensor.transpose(turned[:, 0, :], cos_sb[:, t, :], ident_bf16[:])
-            nc.tensor.transpose(turned[:, 1, :], crossed[t][:], ident_bf16[:])
-            table = keep.tile([P, 2, P], BF16, name="turned_table_%d" % t)
-            nc.scalar.copy(out=table[:], in_=turned[:])
-            turned_tables[t] = table
+        def turn_tables(tiles):
+            turned = banks.tile([P, len(tiles), 2, P], BF16, tag="bank")
+            for n, t in enumerate(tiles):
+                nc.tensor.transpose(turned[:, n, 0, :], cos_sb[:, t, :], ident_bf16[:])
+                nc.tensor.transpose(turned[:, n, 1, :], crossed[t][:], ident_bf16[:])
+            tables = keep.tile([P, len(tiles), 2, P], BF16)
+            nc.scalar.copy(out=tables[:], in_=turned[:])
+            for n, t in enumerate(tiles):
+                turned_tables[t] = tables[:, n, :, :]
 
         def turned_products(t, o, b, shared):
             acc = banks.tile([P, HEADS_PER_BANK, P], F32, tag="bank")
@@ -210,7 +212,7 @@ def tile_attention_pa_kernel(
                 nc.vector.tensor_tensor(
                     out=products[:],
                     in0=acc[:].unsqueeze(1).to_broadcast(shape),
-                    in1=turned_tables[t][:].unsqueeze(2).to_broadcast(shape),
+                    in1=turned_tables[t].unsqueeze(2).to_broadcast(shape),
                     op=ALU.mult,
                 )
             return products
@@ -278,7 +280,7 @@ def tile_attention_pa_kernel(
             shared = (i, b) in SHARED
             products = turned_products(t, o, b, shared)
             following = BANKS_PER_OUTPUT * (len(outputs) - i) - 1 - b
-            lag = min(SHARED_LAG if shared else TURN_LAG, following)
+            lag = min(SHARED_LAG if shared else TURN_LAG + (stored is None), following)
             waiting.append([lag, (t, o, b, products, rotated, stored)])
             bank_done()
 
@@ -296,12 +298,13 @@ def tile_attention_pa_kernel(
                 prepare(t)
             lay_out_factors(nc.scalar.copy, nc.scalar.mul, 2, 3)
             lay_out_factors(nc.scalar.copy, nc.scalar.mul, 3, TOKEN_TILES)
-            for t in sorted({outputs[i][0] for i in TURNED}):
+            turned_tiles = [outputs[i][0] for i in TURNED]
+            for t in turned_tiles:
                 cross_sines(t)
             last = len(outputs) - 1
             for i, (t, o) in enumerate(outputs):
-                if i + 1 in TURNED and outputs[i + 1][0] not in turned_tables:
-                    turn_tables(outputs[i + 1][0])
+                if i + 1 == min(TURNED):
+                    turn_tables(turned_tiles)
                 turned = TURNED.get(i, ())
                 rotated = results.tile([P, HEADS, D], F32, tag="turned" if turned else "rotated")
                 if i in started:

@@ -211,8 +211,8 @@ def tile_attention_pa_kernel(
                 shape = [P, 2, HEADS_PER_BANK, P]
                 nc.vector.tensor_tensor(
                     out=products[:],
-                    in0=acc[:].unsqueeze(1).to_broadcast(shape),
-                    in1=turned_tables[t].unsqueeze(2).to_broadcast(shape),
+                    in0=turned_tables[t].unsqueeze(2).to_broadcast(shape),
+                    in1=acc[:].unsqueeze(1).to_broadcast(shape),
                     op=ALU.mult,
                 )
             return products
@@ -237,8 +237,8 @@ def tile_attention_pa_kernel(
             acc = project(t, BANKS_PER_OUTPUT * o + b)
             nc.vector.tensor_tensor(
                 out=products[:, :, HEADS_PER_BANK * b : HEADS_PER_BANK * (b + 1), :],
-                in0=acc[:].rearrange("p (h d) -> p h d", d=D).unsqueeze(1).to_broadcast(shape),
-                in1=factors[:, t, :, :].unsqueeze(2).to_broadcast(shape),
+                in0=factors[:, t, :, :].unsqueeze(2).to_broadcast(shape),
+                in1=acc[:].rearrange("p (h d) -> p h d", d=D).unsqueeze(1).to_broadcast(shape),
                 op=ALU.mult,
             )
 

from contextlib import ExitStack

import concourse.mybir as mybir
from concourse.masks import make_identity

F32 = mybir.dt.float32
BF16 = mybir.dt.bfloat16
I32 = mybir.dt.int32
U32 = mybir.dt.uint32
U8 = mybir.dt.uint8
FP8X4 = mybir.dt.float8_e4m3fn_x4
FP4X4 = mybir.dt.float4_e2m1fn_x4
ALU = mybir.AluOpType

P = 128
PACK = 4
K_PASS = P * PACK
TOKENS = 1024
HID = 1024
HEADS = 8
D = 128
HALF = D // 2
QKV = 3 * HEADS * D
TOKEN_TILES = TOKENS // P
PASSES = HID // K_PASS
BANK = 512
HEADS_PER_BANK = BANK // D
BANKS_PER_OUTPUT = HEADS // HEADS_PER_BANK

TURNED = {10: (0, 1), 12: (0, 1), 14: (0,), 15: (0,)}
SHARED = ()
TURN_LAG = 3
SHARED_LAG = 11
FLOPS = 2 * TOKENS * HID * QKV


def tile_attention_pa_kernel(
    tc, hidden_states, cos, sin, w_qkv_words, w_qkv_scales, out_0, out_1, out_2
):
    nc = tc.nc

    x_dram = hidden_states[0].rearrange("(p t) k -> p t k", t=TOKEN_TILES)
    cos_dram = cos.rearrange("(p t) d -> p t d", t=TOKEN_TILES)
    sin_dram = sin.rearrange("(p t) d -> p t d", t=TOKEN_TILES)
    rotated_dram = [
        o[0].rearrange("(p t) h d -> p t (h d)", t=TOKEN_TILES) for o in (out_0, out_1)
    ]
    v_dram = out_2[0].rearrange("(p t) h d -> p t (h d)", t=TOKEN_TILES)

    with ExitStack() as ctx:
        keep = ctx.enter_context(tc.tile_pool(name="keep", bufs=1))
        stage = ctx.enter_context(tc.tile_pool(name="stage", bufs=4))
        results = ctx.enter_context(tc.tile_pool(name="results", bufs=4))
        banks = ctx.enter_context(tc.psum_pool(name="banks", bufs=8))

        x_sb = keep.tile([P, TOKEN_TILES, HID], BF16)
        cos_sb = keep.tile([P, TOKEN_TILES, D], BF16)
        sin_sb = keep.tile([P, TOKEN_TILES, D], BF16)
        w_pieces = []
        for first, count in ((0, 1), (1, 1), (2, 2), (4, 2)):
            words = keep.tile([P, PASSES, 2 * BANK * count], U8, align_bytes=64, name="w_words_%d" % first)
            w_pieces.append((first, count, words))
        w_words = {first + b: (words, b) for first, count, words in w_pieces for b in range(count)}
        w_scales = []
        for outputs_in in (1, 2):
            plane = keep.tile([P, PASSES, HEADS * D * outputs_in], U8, align_bytes=64, name="w_scales_%d" % outputs_in)
            nc.vector.memset(plane[:].rearrange("p g n -> p (g n)").bitcast(I32), 0)
            w_scales.append(plane)

        def scale_columns(c, first, last):
            if c < BANKS_PER_OUTPUT:
                return w_scales[0], slice(BANK * c + first, BANK * c + last)
            return w_scales[1], slice(BANK * (c - BANKS_PER_OUTPUT) + first, BANK * (c - BANKS_PER_OUTPUT) + last)

        def load_x(t):
            nc.sync.dma_start(out=x_sb[:, t, :], in_=x_dram[:, t, :])

        def load_words(piece):
            first, count, words = w_pieces[piece]
            nc.sync.dma_start(
                out=words[:].bitcast(I32),
                in_=w_qkv_words[:, :, 2 * BANK * first : 2 * BANK * (first + count)]
                .rearrange("g p n -> p g n")
                .bitcast(I32),
            )

        def load_scales(tile):
            first, last = ((0, HEADS * D), (HEADS * D, QKV))[tile]
            for r in range(4):
                nc.sync.dma_start(
                    out=w_scales[tile][r:P:32, :, :].bitcast(I32),
                    in_=w_qkv_scales[:, r:16:4, first:last].rearrange("g q n -> q g n").bitcast(I32),
                )

        def load_tables(first, last):
            nc.sync.dma_start(out=sin_sb[:, first:last, :], in_=sin_dram[:, first:last, :])
            nc.sync.dma_start(out=cos_sb[:, first:last, :], in_=cos_dram[:, first:last, :])

        load_x(0)
        load_tables(0, 2)
        for t in range(1, 5):
            load_x(t)
        load_scales(0)
        load_words(0)
        for t in range(5, TOKEN_TILES):
            load_x(t)
        load_words(1)
        load_tables(2, TOKEN_TILES)
        load_scales(1)
        load_words(3)
        load_words(2)

        ident = keep.tile([P, P], F32)
        make_identity(nc, ident[:])
        ident_bf16 = keep.tile([P, P], BF16)
        nc.scalar.copy(out=ident_bf16[:], in_=ident[:])
        swap = keep.tile([P, P], F32)
        nc.scalar.copy(out=swap[:, 0:HALF], in_=ident[:, HALF:D])
        nc.scalar.copy(out=swap[:, HALF:D], in_=ident[:, 0:HALF])

        x_codes = keep.tile([P, TOKEN_TILES, PASSES * P], U32, align_bytes=64)
        x_scales = keep.tile([P, TOKEN_TILES, PASSES * P], U8, align_bytes=64)
        factors = keep.tile([P, TOKEN_TILES, 2, D], BF16)

        def prepare(t):
            x_words = x_sb[:, t, :].bitcast(F32)
            xt = banks.tile([P, PASSES, 2, P], F32, tag="bank")
            for g in range(PASSES):
                for u in range(2):
                    nc.tensor.transpose(
                        xt[:, g, u, :], x_words[:, 256 * g + u : 256 * (g + 1) : 2], ident[:]
                    )
            grouped = stage.tile([P, PASSES * P * PACK], BF16, align_bytes=64)
            nc.scalar.copy(
                out=grouped[:].bitcast(F32).rearrange("p (g r u) -> p g r u", g=PASSES, u=2),
                in_=xt[:].rearrange("p g u r -> p g r u"),
            )
            nc.vector.quantize_mx(
                out=x_codes[:, t, :].bitcast(FP8X4), scales=x_scales[:, t, :], in_=grouped[:]
            )

        def lay_out_factors(copy, multiply_by, first, last):
            tiles = slice(first, last)
            copy(out=factors[:, tiles, 0, 0:HALF], in_=cos_sb[:, tiles, 0:HALF])
            multiply_by(factors[:, tiles, 0, HALF:D], sin_sb[:, tiles, 0:HALF], -1.0)
            copy(out=factors[:, tiles, 1, 0:HALF], in_=sin_sb[:, tiles, HALF:D])
            copy(out=factors[:, tiles, 1, HALF:D], in_=cos_sb[:, tiles, HALF:D])

        def project(t, c):
            acc = banks.tile([P, BANK], F32, tag="bank")
            words, at = w_words[c]
            scales, columns = scale_columns(c, 0, BANK)
            for g in range(PASSES):
                nc.tensor.matmul_mx(
                    out=acc[:],
                    lhsT=x_codes[:, t, P * g : P * (g + 1)].bitcast(FP8X4),
                    lhsT_scale=x_scales[:, t, P * g : P * (g + 1)],
                    rhs=words[:, g, 2 * BANK * at : 2 * BANK * (at + 1)].bitcast(FP4X4),
                    rhs_scale=scales[:, g, columns],
                    start=(g == 0),
                    stop=(g == PASSES - 1),
                )
            return acc

        crossed = {}
        turned_tables = {}

        def cross_sines(t):
            row = keep.tile([P, D], BF16, name="crossed_%d" % t)
            nc.scalar.copy(out=row[:, 0:HALF], in_=sin_sb[:, t, HALF:D])
            nc.scalar.mul(out=row[:, HALF:D], in_=sin_sb[:, t, 0:HALF], mul=-1.0)
            crossed[t] = row

        def turn_tables(tiles):
            turned = banks.tile([P, len(tiles), 2, P], BF16, tag="bank")
            for n, t in enumerate(tiles):
                nc.tensor.transpose(turned[:, n, 0, :], cos_sb[:, t, :], ident_bf16[:])
                nc.tensor.transpose(turned[:, n, 1, :], crossed[t][:], ident_bf16[:])
            tables = keep.tile([P, len(tiles), 2, P], BF16)
            nc.scalar.copy(out=tables[:], in_=turned[:])
            for n, t in enumerate(tiles):
                turned_tables[t] = tables[:, n, :, :]

        def turned_products(t, o, b, shared):
            acc = banks.tile([P, HEADS_PER_BANK, P], F32, tag="bank")
            words, at = w_words[BANKS_PER_OUTPUT * o + b]
            for h in range(HEADS_PER_BANK):
                scales, columns = scale_columns(BANKS_PER_OUTPUT * o + b, D * h, D * (h + 1))
                for g in range(PASSES):
                    nc.tensor.matmul_mx(
                        out=acc[:, h, :],
                        lhsT=words[:, g, 2 * (BANK * at + D * h) : 2 * (BANK * at + D * (h + 1))].bitcast(FP4X4),
                        lhsT_scale=scales[:, g, columns],
                        rhs=x_codes[:, t, P * g : P * (g + 1)].bitcast(FP8X4),
                        rhs_scale=x_scales[:, t, P * g : P * (g + 1)],
                        start=(g == 0),
                        stop=(g == PASSES - 1),
                    )
            products = results.tile([P, 2, HEADS_PER_BANK, P], F32, tag="turned_products")
            if shared:
                u = results.tile([P, HEADS_PER_BANK, P], F32)
                nc.scalar.copy(out=u[:], in_=acc[:])
                for engine, source, r in ((nc.vector, acc, 0), (nc.gpsimd, u, 1)):
                    engine.tensor_tensor(
                        out=products[:, r, :, :],
                        in0=source[:],
                        in1=turned_tables[t][:, r, :].unsqueeze(1).to_broadcast([P, HEADS_PER_BANK, P]),
                        op=ALU.mult,
                    )
            else:
                shape = [P, 2, HEADS_PER_BANK, P]
                nc.vector.tensor_tensor(
                    out=products[:],
                    in0=turned_tables[t].unsqueeze(2).to_broadcast(shape),
                    in1=acc[:].unsqueeze(1).to_broadcast(shape),
                    op=ALU.mult,
                )
            return products

        def turn_back(t, o, b, products, rotated, stored):
            total = banks.tile([P, HEADS_PER_BANK, D], F32, tag="bank")
            for h in range(HEADS_PER_BANK):
                nc.tensor.matmul(out=total[:, h, :], lhsT=products[:, 0, h, :], rhs=ident[:],
                                 start=True, stop=False, is_transpose=True)
                nc.tensor.matmul(out=total[:, h, :], lhsT=products[:, 1, h, :], rhs=swap[:],
                                 start=False, stop=True, is_transpose=True)
            first, last = HEADS_PER_BANK * b, HEADS_PER_BANK * (b + 1)
            nc.scalar.copy(out=rotated[:, first:last, :], in_=total[:])
            if stored:
                nc.scalar.dma_start(
                    out=rotated_dram[o][:, t, D * stored[0] : D * stored[1]],
                    in_=rotated[:, stored[0] : stored[1], :].rearrange("p h d -> p (h d)"),
                )

        def multiply(t, o, products, b):
            shape = [P, 2, HEADS_PER_BANK, D]
            acc = project(t, BANKS_PER_OUTPUT * o + b)
            nc.vector.tensor_tensor(
                out=products[:, :, HEADS_PER_BANK * b : HEADS_PER_BANK * (b + 1), :],
                in0=factors[:, t, :, :].unsqueeze(2).to_broadcast(shape),
                in1=acc[:].rearrange("p (h d) -> p h d", d=D).unsqueeze(1).to_broadcast(shape),
                op=ALU.mult,
            )

        def add_and_store(t, o, products, rotated, adder, first, last):
            adder.tensor_tensor(
                out=rotated[:, first:last, :].rearrange("p h (r j) -> p r h j", r=2),
                in0=products[:, :, first:last, 0:HALF],
                in1=products[:, :, first:last, HALF:D],
                op=ALU.add,
            )
            nc.sync.dma_start(
                out=rotated_dram[o][:, t, D * first : D * last],
                in_=rotated[:, first:last, :].rearrange("p h d -> p (h d)"),
            )

        v_pair = []

        def copy_v(t):
            if t % 2 == 0:
                v_pair.append(results.tile([P, 2, HEADS * D], F32, name="v_%d" % t, tag="v"))
            v_sb = v_pair[-1]
            for b in range(BANKS_PER_OUTPUT):
                acc = project(t, BANKS_PER_OUTPUT * 2 + b)
                nc.scalar.copy(out=v_sb[:, t % 2, BANK * b : BANK * (b + 1)], in_=acc[:])
            if t % 2 == 1:
                nc.scalar.dma_start(out=v_dram[:, t - 1 : t + 1, :], in_=v_sb[:])

        waiting = []

        def bank_done():
            for entry in waiting:
                entry[0] -= 1
            for entry in [e for e in waiting if e[0] < 0]:
                waiting.remove(entry)
                turn_back(*entry[1])

        def start_turned(i, b, rotated, stored):
            t, o = outputs[i]
            shared = (i, b) in SHARED
            products = turned_products(t, o, b, shared)
            following = BANKS_PER_OUTPUT * (len(outputs) - i) - 1 - b
            lag = min(SHARED_LAG if shared else TURN_LAG + (stored is None), following)
            waiting.append([lag, (t, o, b, products, rotated, stored)])
            bank_done()

        outputs = [(t, o) for o in range(2) for t in range(TOKEN_TILES)]
        with tc.manual_schedule():
            prepare(0)
            lay_out_factors(nc.vector.tensor_copy, nc.vector.tensor_scalar_mul, 0, 2)
            for t in range(1, 5):
                prepare(t)
            started = {}
            for i in range(2):
                started[i] = results.tile([P, 2, HEADS, D], F32, name="products_%d" % i, tag="products")
                multiply(i, 0, started[i], 0)
            for t in range(5, TOKEN_TILES):
                prepare(t)
            lay_out_factors(nc.scalar.copy, nc.scalar.mul, 2, 3)
            lay_out_factors(nc.scalar.copy, nc.scalar.mul, 3, TOKEN_TILES)
            turned_tiles = [outputs[i][0] for i in TURNED]
            for t in turned_tiles:
                cross_sines(t)
            last = len(outputs) - 1
            for i, (t, o) in enumerate(outputs):
                if i + 1 == min(TURNED):
                    turn_tables(turned_tiles)
                turned = TURNED.get(i, ())
                rotated = results.tile([P, HEADS, D], F32, tag="turned" if turned else "rotated")
                if i in started:
                    products = started[i]
                elif len(turned) < BANKS_PER_OUTPUT:
                    products = results.tile([P, 2, HEADS, D], F32, tag="products")
                by_bank = len(turned) == 1 or i == last - 1
                for b in range(BANKS_PER_OUTPUT):
                    heads = (HEADS_PER_BANK * b, HEADS_PER_BANK * (b + 1))
                    if b in turned:
                        whole = len(turned) == BANKS_PER_OUTPUT
                        stored = heads if not whole else (0, HEADS) if b == BANKS_PER_OUTPUT - 1 else None
                        start_turned(i, b, rotated, stored)
                        continue
                    if b > 0 or i not in started:
                        multiply(t, o, products, b)
                        bank_done()
                    if by_bank:
                        add_and_store(t, o, products, rotated, nc.vector if i == last else nc.gpsimd, *heads)
                if not turned and not by_bank:
                    add_and_store(t, o, products, rotated, nc.gpsimd, 0, HEADS)
                if 2 <= i < TOKEN_TILES + 2:
                    copy_v(i - 2)
